import numpy as np
import ml_dtypes


def mxq(x, axis, fmt="e4m3"):
    dtype, down = {"e4m3": (ml_dtypes.float8_e4m3fn, 7), "e5m2": (ml_dtypes.float8_e5m2, 14)}[fmt]
    v = np.moveaxis(np.asarray(x, np.float32).astype(ml_dtypes.bfloat16).astype(np.float64), axis, -1)
    blocks = v.reshape(v.shape[:-1] + (-1, 32))
    amax = np.abs(blocks).max(-1, keepdims=True)
    byte = np.maximum(np.where(amax > 0, np.frexp(amax)[1] - 1 + 127, 0) - down, 1)
    scale = np.exp2(byte - 127.0)
    codes = (blocks / scale).astype(np.float32).astype(dtype).astype(np.float64)
    return np.moveaxis((codes * scale).reshape(v.shape), -1, axis)


WIDE = False


def mx_kscale(k):
    if not WIDE:
        return np.ones(k)
    levels = np.array([10, -10, 5, -5, 0])
    a = np.random.permutation(np.resize(levels, k // 512 * 4)).reshape(k // 512, 4)
    idx = np.arange(k)
    return np.exp2(a[idx // 512, idx % 128 // 32])


BF16 = ml_dtypes.bfloat16


def bf(x):
    return np.asarray(x, np.float32).astype(BF16)


def f64(x):
    return np.asarray(x).astype(np.float64)


E2M1 = np.array([0.0, 0.5, 1.0, 1.5, 2.0, 3.0, 4.0, 6.0, -0.0, -0.5, -1.0, -1.5, -2.0, -3.0, -4.0, -6.0])


def pack_weight(w, fmt):
    k, n = w.shape
    w = f64(bf(w)).reshape(k // 32, 32, n)
    amax = np.abs(w).max(1)
    if fmt == "e4m3":
        byte = np.frexp(amax)[1] - 1 + 127 - 7
    else:
        mant, ex = np.frexp(amax / 6.0)
        byte = np.where(mant > 0.5, ex, ex - 1) + 127
    byte = np.clip(np.where(amax > 0, byte, 1), 1, 254)
    scaled = (w * np.exp2(127.0 - byte)[:, None, :]).reshape(k, n).astype(np.float32)
    by_word = np.ascontiguousarray(scaled.reshape(k // 512, 128, 4, n).transpose(0, 1, 3, 2))
    if fmt == "e4m3":
        words = by_word.astype(ml_dtypes.float8_e4m3fn).view(np.uint8)
    else:
        c = by_word.astype(ml_dtypes.float4_e2m1fn).view(np.uint8) & 0xF
        words = c[..., 0::2] | (c[..., 1::2] << 4)
    return np.ascontiguousarray(words), np.ascontiguousarray(byte.astype(np.uint8).reshape(k // 512, 16, n))


def unpack_weight(words, scales, fmt):
    g, p, n, _ = words.shape
    if fmt == "e4m3":
        vals = np.ascontiguousarray(words).view(ml_dtypes.float8_e4m3fn).astype(np.float64)
    else:
        nib = np.empty((g, p, n, 4), np.uint8)
        nib[..., 0::2] = words & 0xF
        nib[..., 1::2] = words >> 4
        vals = E2M1[nib]
    vals = vals * np.repeat(np.exp2(scales.astype(np.float64) - 127.0), 8, axis=1)[..., None]
    return vals.transpose(0, 1, 3, 2).reshape(g * 512, n)

def pack4(w):
    words, scales = pack_weight(w, "e2m1")
    return words.reshape(words.shape[0], 128, -1), scales


def unpack4(words, scales):
    return unpack_weight(words.reshape(words.shape[0], 128, -1, 2), scales, "e2m1")


B, N, D, A = 1, 128, 4096, 128
K = D + D
NB = N // A


def setup_inputs():
    st = mx_kscale(K)
    s, t = st[:D], st[D:]
    data = bf(np.random.standard_normal((B, N, D)) * 2.0 * s)
    pooled = bf(np.random.standard_normal((B, N, A)) * 0.37 / np.sqrt(NB))
    W_abs = bf(np.random.standard_normal((A, D)) * 3.0 * np.sqrt(NB / A) * t)
    words, scales = pack4(np.random.standard_normal((K, D)) * 0.5 / np.sqrt(D) / st[:, None])
    return {"data": data,
            "pooled": pooled,
            "W_abs": W_abs,
            "W_merge_words": words,
            "W_merge_scales": scales}


def reference(data, pooled, W_abs, W_merge_words, W_merge_scales):
    abstract = f64(pooled) @ f64(W_abs)
    x = np.concatenate([f64(data), abstract], axis=-1)
    return mxq(x, 2, "e4m3") @ unpack4(W_merge_words, W_merge_scales)

@@ -1,0 +1,174 @@
+import concourse.mybir as mybir
+from concourse.masks import make_identity
+
+BF16 = mybir.dt.bfloat16
+F32 = mybir.dt.float32
+I32 = mybir.dt.int32
+U8 = mybir.dt.uint8
+U32 = mybir.dt.uint32
+FP8X4 = mybir.dt.float8_e4m3fn_x4
+FP4X4 = mybir.dt.float4_e2m1fn_x4
+
+P = 128
+TOKENS = 128
+A = 128
+D = 4096
+PACK = 4
+K_PASS = P * PACK
+DATA_PASSES = D // K_PASS
+PASSES = 2 * DATA_PASSES
+N_TILE = 512
+N_TILES = D // N_TILE
+X_COLS = TOKENS * PACK
+FP4_BYTES = 2
+
+GROUP_PASSES = 8
+SCALE_DMA_PASSES = 4
+WORD_BUFS = 8
+MEMSET_PASSES = 4
+
+FLOPS = 2 * TOKENS * (2 * D) * D + 2 * TOKENS * A * D
+
+
+def tile_abstraction_pb_k_kernel(
+    tc, data, pooled, W_abs, W_merge_words, W_merge_scales, out
+):
+    nc = tc.nc
+    data_rows = data.flatten_outer_dims()
+    pooled_rows = pooled.flatten_outer_dims()
+    out_rows = out.flatten_outer_dims()
+    scale_rows = W_merge_scales.bitcast(I32)
+
+    with tc.tile_pool(name="keep", bufs=1) as keep, tc.tile_pool(
+        name="ring", bufs=WORD_BUFS
+    ) as ring, tc.tile_pool(name="results", bufs=N_TILES) as results, tc.psum_pool(
+        name="psum", bufs=N_TILES
+    ) as psum, tc.manual_schedule():
+
+        pooled_sb = keep.tile([TOKENS, A], BF16)
+        nc.sync.dma_start(out=pooled_sb[:], in_=pooled_rows)
+        data_sb = keep.tile([TOKENS, D], BF16)
+        nc.sync.dma_start(out=data_sb[:], in_=data_rows)
+        w_abs_sb = keep.tile([A, D], BF16)
+        nc.sync.dma_start(out=w_abs_sb[:], in_=W_abs)
+
+        ident_f32 = keep.tile([P, P], F32)
+        make_identity(nc, ident_f32[:])
+        ident_bf16 = keep.tile([P, P], BF16)
+        nc.vector.tensor_copy(out=ident_bf16[:], in_=ident_f32[:])
+
+        w_planes = keep.tile([P, PASSES, D], U8, align_bytes=64)
+        for g in range(0, PASSES, MEMSET_PASSES):
+            nc.vector.memset(w_planes[:, g : g + MEMSET_PASSES, :].bitcast(I32), 0)
+
+        def load_scales(first_pass):
+            for g in range(first_pass, first_pass + GROUP_PASSES, SCALE_DMA_PASSES):
+                for b in range(2):
+                    for r in range(4):
+                        nc.sync.dma_start(
+                            out=w_planes[
+                                32 * b + r : P : 64, g : g + SCALE_DMA_PASSES, :
+                            ].bitcast(I32),
+                            in_=scale_rows[
+                                g : g + SCALE_DMA_PASSES, 4 * b + r : 16 : 8, :
+                            ].rearrange("g q n -> q g n"),
+                        )
+
+        w_words = {}
+
+        def load_pass(g):
+            if g % GROUP_PASSES == 0:
+                load_scales(g)
+            w_words[g] = ring.tile([P, FP4_BYTES * D], U8, align_bytes=64, name="w_words")
+            nc.sync.dma_start(
+                out=w_words[g][:].bitcast(I32), in_=W_merge_words[g].bitcast(I32)
+            )
+
+        for g in range(WORD_BUFS):
+            load_pass(g)
+
+        x_grouped = keep.tile([P, PASSES * X_COLS], BF16, align_bytes=64)
+        x_codes = keep.tile([P, PASSES * TOKENS], U32, align_bytes=64)
+        x_scales = keep.tile([P, PASSES * TOKENS], U8, align_bytes=64)
+
+        def quantise_half(first_pass):
+            nc.vector.quantize_mx(
+                out=x_codes[
+                    :, first_pass * TOKENS : (first_pass + DATA_PASSES) * TOKENS
+                ].bitcast(FP8X4),
+                scales=x_scales[:, first_pass * TOKENS : (first_pass + DATA_PASSES) * TOKENS],
+                in_=x_grouped[:, first_pass * X_COLS : (first_pass + DATA_PASSES) * X_COLS],
+            )
+
+        pooled_t_ps = psum.tile([A, TOKENS], BF16, tag="bank")
+        nc.tensor.transpose(pooled_t_ps[:], pooled_sb[:], ident_bf16[:])
+        pooled_t = keep.tile([A, TOKENS], BF16)
+        nc.scalar.copy(out=pooled_t[:], in_=pooled_t_ps[:])
+
+        data_words = data_sb[:].bitcast(F32)
+        words_per_pass = K_PASS // 2
+        for pair in range(DATA_PASSES // 2):
+            data_t = psum.tile([P, 2, 2, TOKENS], F32, tag="bank")
+            for j in range(2):
+                g = 2 * pair + j
+                for u in range(2):
+                    nc.tensor.transpose(
+                        data_t[:, j, u, :],
+                        data_words[:, words_per_pass * g + u : words_per_pass * (g + 1) : 2],
+                        ident_f32[:],
+                    )
+            nc.scalar.copy(
+                out=x_grouped[:, 2 * pair * X_COLS : (2 * pair + 2) * X_COLS]
+                .bitcast(F32)
+                .rearrange("p (j r u) -> p j r u", j=2, u=2),
+                in_=data_t[:].rearrange("p j u r -> p j r u"),
+            )
+        quantise_half(0)
+
+        for j in range(DATA_PASSES):
+            abstract_t = psum.tile([P, PACK, TOKENS], F32, tag="bank")
+            for t in range(PACK):
+                nc.tensor.matmul(
+                    abstract_t[:, t, :],
+                    lhsT=w_abs_sb[:, K_PASS * j + t : K_PASS * (j + 1) : PACK],
+                    rhs=pooled_t[:],
+                    start=True,
+                    stop=True,
+                )
+            g = DATA_PASSES + j
+            grouped = x_grouped[:, g * X_COLS : (g + 1) * X_COLS].rearrange(
+                "p (r t) -> p r t", t=PACK
+            )
+            if j % 2 == 0:
+                nc.scalar.copy(out=grouped, in_=abstract_t[:].rearrange("p t r -> p r t"))
+            else:
+                nc.vector.tensor_copy(out=grouped, in_=abstract_t[:].rearrange("p t r -> p r t"))
+        quantise_half(DATA_PASSES)
+
+        acc = [
+            psum.tile([TOKENS, N_TILE], F32, tag="bank", name="acc%d" % n)
+            for n in range(N_TILES)
+        ]
+        for g in range(PASSES):
+            for n in range(N_TILES):
+                nc.tensor.matmul_mx(
+                    out=acc[n][:],
+                    lhsT=x_codes[:, g * TOKENS : (g + 1) * TOKENS].bitcast(FP8X4),
+                    lhsT_scale=x_scales[:, g * TOKENS : (g + 1) * TOKENS],
+                    rhs=w_words[g][
+                        :, FP4_BYTES * N_TILE * n : FP4_BYTES * N_TILE * (n + 1)
+                    ].bitcast(FP4X4),
+                    rhs_scale=w_planes[:, g, N_TILE * n : N_TILE * (n + 1)],
+                    start=(g == 0),
+                    stop=(g == PASSES - 1),
+                )
+            if g + WORD_BUFS < PASSES:
+                load_pass(g + WORD_BUFS)
+
+        for n in range(N_TILES):
+            result = results.tile([TOKENS, N_TILE], F32)
+            if n % 2 == 0:
+                nc.scalar.copy(out=result[:], in_=acc[n][:])
+            else:
+                nc.vector.tensor_copy(out=result[:], in_=acc[n][:])
+            nc.sync.dma_start(out=out_rows[:, N_TILE * n : N_TILE * (n + 1)], in_=result[:])

@@ -25,7 +25,6 @@ FP4_BYTES = 2
 GROUP_PASSES = 8
 SCALE_DMA_PASSES = 4
 WORD_BUFS = 8
-MEMSET_PASSES = 4
 
 FLOPS = 2 * TOKENS * (2 * D) * D + 2 * TOKENS * A * D
 
@@ -57,18 +56,19 @@ def tile_abstraction_pb_k_kernel(
         ident_bf16 = keep.tile([P, P], BF16)
         nc.vector.tensor_copy(out=ident_bf16[:], in_=ident_f32[:])
 
-        w_planes = keep.tile([P, PASSES, D], U8, align_bytes=64)
-        for g in range(0, PASSES, MEMSET_PASSES):
-            nc.vector.memset(w_planes[:, g : g + MEMSET_PASSES, :].bitcast(I32), 0)
+        w_planes = [
+            keep.tile([P, SCALE_DMA_PASSES, D], U8, align_bytes=64, name="w_planes%d" % c)
+            for c in range(PASSES // SCALE_DMA_PASSES)
+        ]
+        for planes in w_planes:
+            nc.vector.memset(planes[:].bitcast(I32), 0)
 
         def load_scales(first_pass):
             for g in range(first_pass, first_pass + GROUP_PASSES, SCALE_DMA_PASSES):
                 for b in range(2):
                     for r in range(4):
                         nc.sync.dma_start(
-                            out=w_planes[
-                                32 * b + r : P : 64, g : g + SCALE_DMA_PASSES, :
-                            ].bitcast(I32),
+                            out=w_planes[g // SCALE_DMA_PASSES][32 * b + r : P : 64, :, :].bitcast(I32),
                             in_=scale_rows[
                                 g : g + SCALE_DMA_PASSES, 4 * b + r : 16 : 8, :
                             ].rearrange("g q n -> q g n"),
@@ -158,7 +158,9 @@ def tile_abstraction_pb_k_kernel(
                     rhs=w_words[g][
                         :, FP4_BYTES * N_TILE * n : FP4_BYTES * N_TILE * (n + 1)
                     ].bitcast(FP4X4),
-                    rhs_scale=w_planes[:, g, N_TILE * n : N_TILE * (n + 1)],
+                    rhs_scale=w_planes[g // SCALE_DMA_PASSES][
+                        :, g % SCALE_DMA_PASSES, N_TILE * n : N_TILE * (n + 1)
+                    ],
                     start=(g == 0),
                     stop=(g == PASSES - 1),
                 )

@@ -23,7 +23,6 @@ X_COLS = TOKENS * PACK
 FP4_BYTES = 2
 
 GROUP_PASSES = 8
-SCALE_DMA_PASSES = 4
 WORD_BUFS = 8
 
 FLOPS = 2 * TOKENS * (2 * D) * D + 2 * TOKENS * A * D
@@ -56,23 +55,29 @@ def tile_abstraction_pb_k_kernel(
         ident_bf16 = keep.tile([P, P], BF16)
         nc.vector.tensor_copy(out=ident_bf16[:], in_=ident_f32[:])
 
-        w_planes = [
-            keep.tile([P, SCALE_DMA_PASSES, D], U8, align_bytes=64, name="w_planes%d" % c)
-            for c in range(PASSES // SCALE_DMA_PASSES)
-        ]
-        for planes in w_planes:
-            nc.vector.memset(planes[:].bitcast(I32), 0)
+        w_plane = {}
+        plane_tiles = {}
+        for first_pass in range(0, PASSES, GROUP_PASSES):
+            for start, count in ((first_pass, GROUP_PASSES - 1), (first_pass + GROUP_PASSES - 1, 1)):
+                planes = keep.tile([P, count, D], U8, align_bytes=64, name="planes%d" % start)
+                nc.vector.memset(planes[:].bitcast(I32), 0)
+                plane_tiles[start] = planes
+                for i in range(count):
+                    w_plane[start + i] = planes[:, i, :]
+
+        def load_scale_rows(start, count):
+            for b in range(2):
+                for r in range(4):
+                    nc.sync.dma_start(
+                        out=plane_tiles[start][32 * b + r : P : 64, :, :].bitcast(I32),
+                        in_=scale_rows[start : start + count, 4 * b + r : 16 : 8, :].rearrange(
+                            "g q n -> q g n"
+                        ),
+                    )
 
         def load_scales(first_pass):
-            for g in range(first_pass, first_pass + GROUP_PASSES, SCALE_DMA_PASSES):
-                for b in range(2):
-                    for r in range(4):
-                        nc.sync.dma_start(
-                            out=w_planes[g // SCALE_DMA_PASSES][32 * b + r : P : 64, :, :].bitcast(I32),
-                            in_=scale_rows[
-                                g : g + SCALE_DMA_PASSES, 4 * b + r : 16 : 8, :
-                            ].rearrange("g q n -> q g n"),
-                        )
+            load_scale_rows(first_pass, GROUP_PASSES - 1)
+            load_scale_rows(first_pass + GROUP_PASSES - 1, 1)
 
         w_words = {}
 
@@ -158,9 +163,7 @@ def tile_abstraction_pb_k_kernel(
                     rhs=w_words[g][
                         :, FP4_BYTES * N_TILE * n : FP4_BYTES * N_TILE * (n + 1)
                     ].bitcast(FP4X4),
-                    rhs_scale=w_planes[g // SCALE_DMA_PASSES][
-                        :, g % SCALE_DMA_PASSES, N_TILE * n : N_TILE * (n + 1)
-                    ],
+                    rhs_scale=w_plane[g][:, N_TILE * n : N_TILE * (n + 1)],
                     start=(g == 0),
                     stop=(g == PASSES - 1),
                 )

@@ -24,6 +24,8 @@ FP4_BYTES = 2
 
 GROUP_PASSES = 8
 WORD_BUFS = 8
+TAPER_PASSES = 3
+HALF_TILES = N_TILES // 2
 
 FLOPS = 2 * TOKENS * (2 * D) * D + 2 * TOKENS * A * D
 
@@ -79,18 +81,27 @@ def tile_abstraction_pb_k_kernel(
             load_scale_rows(first_pass, GROUP_PASSES - 1)
             load_scale_rows(first_pass + GROUP_PASSES - 1, 1)
 
+        pieces = [(g, 0, N_TILES) for g in range(PASSES - TAPER_PASSES)]
+        for first_bank in range(0, N_TILES, HALF_TILES):
+            pieces.extend(
+                [(g, first_bank, HALF_TILES) for g in range(PASSES - TAPER_PASSES, PASSES)]
+            )
         w_words = {}
 
-        def load_pass(g):
+        def load_piece(i):
+            g, first_bank, banks = pieces[i]
             if g % GROUP_PASSES == 0:
                 load_scales(g)
-            w_words[g] = ring.tile([P, FP4_BYTES * D], U8, align_bytes=64, name="w_words")
+            first_byte = FP4_BYTES * N_TILE * first_bank
+            n_bytes = FP4_BYTES * N_TILE * banks
+            w_words[i] = ring.tile([P, n_bytes], U8, align_bytes=64, name="w_words")
             nc.sync.dma_start(
-                out=w_words[g][:].bitcast(I32), in_=W_merge_words[g].bitcast(I32)
+                out=w_words[i][:].bitcast(I32),
+                in_=W_merge_words[g][:, first_byte : first_byte + n_bytes].bitcast(I32),
             )
 
-        for g in range(WORD_BUFS):
-            load_pass(g)
+        for i in range(WORD_BUFS):
+            load_piece(i)
 
         x_grouped = keep.tile([P, PASSES * X_COLS], BF16, align_bytes=64)
         x_codes = keep.tile([P, PASSES * TOKENS], U32, align_bytes=64)
@@ -154,26 +165,30 @@ def tile_abstraction_pb_k_kernel(
             psum.tile([TOKENS, N_TILE], F32, tag="bank", name="acc%d" % n)
             for n in range(N_TILES)
         ]
-        for g in range(PASSES):
-            for n in range(N_TILES):
+        for i in range(len(pieces)):
+            g, first_bank, banks = pieces[i]
+            for j in range(banks):
+                n = first_bank + j
                 nc.tensor.matmul_mx(
                     out=acc[n][:],
                     lhsT=x_codes[:, g * TOKENS : (g + 1) * TOKENS].bitcast(FP8X4),
                     lhsT_scale=x_scales[:, g * TOKENS : (g + 1) * TOKENS],
-                    rhs=w_words[g][
-                        :, FP4_BYTES * N_TILE * n : FP4_BYTES * N_TILE * (n + 1)
+                    rhs=w_words[i][
+                        :, FP4_BYTES * N_TILE * j : FP4_BYTES * N_TILE * (j + 1)
                     ].bitcast(FP4X4),
                     rhs_scale=w_plane[g][:, N_TILE * n : N_TILE * (n + 1)],
                     start=(g == 0),
                     stop=(g == PASSES - 1),
                 )
-            if g + WORD_BUFS < PASSES:
-                load_pass(g + WORD_BUFS)
-
-        for n in range(N_TILES):
-            result = results.tile([TOKENS, N_TILE], F32)
-            if n % 2 == 0:
-                nc.scalar.copy(out=result[:], in_=acc[n][:])
-            else:
-                nc.vector.tensor_copy(out=result[:], in_=acc[n][:])
-            nc.sync.dma_start(out=out_rows[:, N_TILE * n : N_TILE * (n + 1)], in_=result[:])
+            if i + WORD_BUFS < len(pieces):
+                load_piece(i + WORD_BUFS)
+            if g == PASSES - 1:
+                for n in range(first_bank, first_bank + banks):
+                    result = results.tile([TOKENS, N_TILE], F32)
+                    if n % 2 == 0:
+                        nc.scalar.copy(out=result[:], in_=acc[n][:])
+                    else:
+                        nc.vector.tensor_copy(out=result[:], in_=acc[n][:])
+                    nc.sync.dma_start(
+                        out=out_rows[:, N_TILE * n : N_TILE * (n + 1)], in_=result[:]
+                    )

@@ -22,7 +22,7 @@ N_TILES = D // N_TILE
 X_COLS = TOKENS * PACK
 FP4_BYTES = 2
 
-GROUP_PASSES = 8
+LEAD_PASSES = 2
 WORD_BUFS = 8
 TAPER_PASSES = 3
 HALF_TILES = N_TILES // 2
@@ -59,13 +59,12 @@ def tile_abstraction_pb_k_kernel(
 
         w_plane = {}
         plane_tiles = {}
-        for first_pass in range(0, PASSES, GROUP_PASSES):
-            for start, count in ((first_pass, GROUP_PASSES - 1), (first_pass + GROUP_PASSES - 1, 1)):
-                planes = keep.tile([P, count, D], U8, align_bytes=64, name="planes%d" % start)
-                nc.vector.memset(planes[:].bitcast(I32), 0)
-                plane_tiles[start] = planes
-                for i in range(count):
-                    w_plane[start + i] = planes[:, i, :]
+        for start, count in ((0, PASSES - 1), (PASSES - 1, 1)):
+            planes = keep.tile([P, count, D], U8, align_bytes=64, name="planes%d" % start)
+            nc.vector.memset(planes[:].bitcast(I32), 0)
+            plane_tiles[start] = planes
+            for i in range(count):
+                w_plane[start + i] = planes[:, i, :]
 
         def load_scale_rows(start, count):
             for b in range(2):
@@ -77,9 +76,9 @@ def tile_abstraction_pb_k_kernel(
                         ),
                     )
 
-        def load_scales(first_pass):
-            load_scale_rows(first_pass, GROUP_PASSES - 1)
-            load_scale_rows(first_pass + GROUP_PASSES - 1, 1)
+        def load_scales():
+            load_scale_rows(0, PASSES - 1)
+            load_scale_rows(PASSES - 1, 1)
 
         pieces = [(g, 0, N_TILES) for g in range(PASSES - TAPER_PASSES)]
         for first_bank in range(0, N_TILES, HALF_TILES):
@@ -90,8 +89,6 @@ def tile_abstraction_pb_k_kernel(
 
         def load_piece(i):
             g, first_bank, banks = pieces[i]
-            if g % GROUP_PASSES == 0:
-                load_scales(g)
             first_byte = FP4_BYTES * N_TILE * first_bank
             n_bytes = FP4_BYTES * N_TILE * banks
             w_words[i] = ring.tile([P, n_bytes], U8, align_bytes=64, name="w_words")
@@ -101,6 +98,8 @@ def tile_abstraction_pb_k_kernel(
             )
 
         for i in range(WORD_BUFS):
+            if i == LEAD_PASSES:
+                load_scales()
             load_piece(i)
 
         x_grouped = keep.tile([P, PASSES * X_COLS], BF16, align_bytes=64)

@@ -22,7 +22,8 @@ N_TILES = D // N_TILE
 X_COLS = TOKENS * PACK
 FP4_BYTES = 2
 
-LEAD_PASSES = 2
+LEAD_PASSES = 6
+PLANE_TILES = ((0, LEAD_PASSES), (LEAD_PASSES, PASSES - 1 - LEAD_PASSES), (PASSES - 1, 1))
 WORD_BUFS = 8
 TAPER_PASSES = 3
 HALF_TILES = N_TILES // 2
@@ -59,7 +60,7 @@ def tile_abstraction_pb_k_kernel(
 
         w_plane = {}
         plane_tiles = {}
-        for start, count in ((0, PASSES - 1), (PASSES - 1, 1)):
+        for start, count in PLANE_TILES:
             planes = keep.tile([P, count, D], U8, align_bytes=64, name="planes%d" % start)
             nc.vector.memset(planes[:].bitcast(I32), 0)
             plane_tiles[start] = planes
@@ -77,8 +78,8 @@ def tile_abstraction_pb_k_kernel(
                     )
 
         def load_scales():
-            load_scale_rows(0, PASSES - 1)
-            load_scale_rows(PASSES - 1, 1)
+            for start, count in PLANE_TILES:
+                load_scale_rows(start, count)
 
         pieces = [(g, 0, N_TILES) for g in range(PASSES - TAPER_PASSES)]
         for first_bank in range(0, N_TILES, HALF_TILES):

@@ -68,8 +68,8 @@ def tile_abstraction_pb_k_kernel(
                 w_plane[start + i] = planes[:, i, :]
 
         def load_scale_rows(start, count):
-            for b in range(2):
-                for r in range(4):
+            for r in range(4):
+                for b in range(2):
                     nc.sync.dma_start(
                         out=plane_tiles[start][32 * b + r : P : 64, :, :].bitcast(I32),
                         in_=scale_rows[start : start + count, 4 * b + r : 16 : 8, :].rearrange(

import concourse.mybir as mybir
from concourse.masks import make_identity

BF16 = mybir.dt.bfloat16
F32 = mybir.dt.float32
I32 = mybir.dt.int32
U8 = mybir.dt.uint8
U32 = mybir.dt.uint32
FP8X4 = mybir.dt.float8_e4m3fn_x4
FP4X4 = mybir.dt.float4_e2m1fn_x4

P = 128
TOKENS = 128
A = 128
D = 4096
PACK = 4
K_PASS = P * PACK
DATA_PASSES = D // K_PASS
PASSES = 2 * DATA_PASSES
N_TILE = 512
N_TILES = D // N_TILE
X_COLS = TOKENS * PACK
FP4_BYTES = 2

LEAD_PASSES = 6
PLANE_TILES = ((0, LEAD_PASSES), (LEAD_PASSES, PASSES - 1 - LEAD_PASSES), (PASSES - 1, 1))
WORD_BUFS = 8
TAPER_PASSES = 3
HALF_TILES = N_TILES // 2

FLOPS = 2 * TOKENS * (2 * D) * D + 2 * TOKENS * A * D


def tile_abstraction_pb_k_kernel(
    tc, data, pooled, W_abs, W_merge_words, W_merge_scales, out
):
    nc = tc.nc
    data_rows = data.flatten_outer_dims()
    pooled_rows = pooled.flatten_outer_dims()
    out_rows = out.flatten_outer_dims()
    scale_rows = W_merge_scales.bitcast(I32)

    with tc.tile_pool(name="keep", bufs=1) as keep, tc.tile_pool(
        name="ring", bufs=WORD_BUFS
    ) as ring, tc.tile_pool(name="results", bufs=N_TILES) as results, tc.psum_pool(
        name="psum", bufs=N_TILES
    ) as psum, tc.manual_schedule():

        pooled_sb = keep.tile([TOKENS, A], BF16)
        nc.sync.dma_start(out=pooled_sb[:], in_=pooled_rows)
        data_sb = keep.tile([TOKENS, D], BF16)
        nc.sync.dma_start(out=data_sb[:], in_=data_rows)
        w_abs_sb = keep.tile([A, D], BF16)
        nc.sync.dma_start(out=w_abs_sb[:], in_=W_abs)

        ident_f32 = keep.tile([P, P], F32)
        make_identity(nc, ident_f32[:])
        ident_bf16 = keep.tile([P, P], BF16)
        nc.vector.tensor_copy(out=ident_bf16[:], in_=ident_f32[:])

        w_plane = {}
        plane_tiles = {}
        for start, count in PLANE_TILES:
            planes = keep.tile([P, count, D], U8, align_bytes=64, name="planes%d" % start)
            nc.vector.memset(planes[:].bitcast(I32), 0)
            plane_tiles[start] = planes
            for i in range(count):
                w_plane[start + i] = planes[:, i, :]

        def load_scale_rows(start, count):
            for r in range(4):
                for b in range(2):
                    nc.sync.dma_start(
                        out=plane_tiles[start][32 * b + r : P : 64, :, :].bitcast(I32),
                        in_=scale_rows[start : start + count, 4 * b + r : 16 : 8, :].rearrange(
                            "g q n -> q g n"
                        ),
                    )

        def load_scales():
            for start, count in PLANE_TILES:
                load_scale_rows(start, count)

        pieces = [(g, 0, N_TILES) for g in range(PASSES - TAPER_PASSES)]
        for first_bank in range(0, N_TILES, HALF_TILES):
            pieces.extend(
                [(g, first_bank, HALF_TILES) for g in range(PASSES - TAPER_PASSES, PASSES)]
            )
        w_words = {}

        def load_piece(i):
            g, first_bank, banks = pieces[i]
            first_byte = FP4_BYTES * N_TILE * first_bank
            n_bytes = FP4_BYTES * N_TILE * banks
            w_words[i] = ring.tile([P, n_bytes], U8, align_bytes=64, name="w_words")
            nc.sync.dma_start(
                out=w_words[i][:].bitcast(I32),
                in_=W_merge_words[g][:, first_byte : first_byte + n_bytes].bitcast(I32),
            )

        for i in range(WORD_BUFS):
            if i == LEAD_PASSES:
                load_scales()
            load_piece(i)

        x_grouped = keep.tile([P, PASSES * X_COLS], BF16, align_bytes=64)
        x_codes = keep.tile([P, PASSES * TOKENS], U32, align_bytes=64)
        x_scales = keep.tile([P, PASSES * TOKENS], U8, align_bytes=64)

        def quantise_half(first_pass):
            nc.vector.quantize_mx(
                out=x_codes[
                    :, first_pass * TOKENS : (first_pass + DATA_PASSES) * TOKENS
                ].bitcast(FP8X4),
                scales=x_scales[:, first_pass * TOKENS : (first_pass + DATA_PASSES) * TOKENS],
                in_=x_grouped[:, first_pass * X_COLS : (first_pass + DATA_PASSES) * X_COLS],
            )

        pooled_t_ps = psum.tile([A, TOKENS], BF16, tag="bank")
        nc.tensor.transpose(pooled_t_ps[:], pooled_sb[:], ident_bf16[:])
        pooled_t = keep.tile([A, TOKENS], BF16)
        nc.scalar.copy(out=pooled_t[:], in_=pooled_t_ps[:])

        data_words = data_sb[:].bitcast(F32)
        words_per_pass = K_PASS // 2
        for pair in range(DATA_PASSES // 2):
            data_t = psum.tile([P, 2, 2, TOKENS], F32, tag="bank")
            for j in range(2):
                g = 2 * pair + j
                for u in range(2):
                    nc.tensor.transpose(
                        data_t[:, j, u, :],
                        data_words[:, words_per_pass * g + u : words_per_pass * (g + 1) : 2],
                        ident_f32[:],
                    )
            nc.scalar.copy(
                out=x_grouped[:, 2 * pair * X_COLS : (2 * pair + 2) * X_COLS]
                .bitcast(F32)
                .rearrange("p (j r u) -> p j r u", j=2, u=2),
                in_=data_t[:].rearrange("p j u r -> p j r u"),
            )
        quantise_half(0)

        for j in range(DATA_PASSES):
            abstract_t = psum.tile([P, PACK, TOKENS], F32, tag="bank")
            for t in range(PACK):
                nc.tensor.matmul(
                    abstract_t[:, t, :],
                    lhsT=w_abs_sb[:, K_PASS * j + t : K_PASS * (j + 1) : PACK],
                    rhs=pooled_t[:],
                    start=True,
                    stop=True,
                )
            g = DATA_PASSES + j
            grouped = x_grouped[:, g * X_COLS : (g + 1) * X_COLS].rearrange(
                "p (r t) -> p r t", t=PACK
            )
            if j % 2 == 0:
                nc.scalar.copy(out=grouped, in_=abstract_t[:].rearrange("p t r -> p r t"))
            else:
                nc.vector.tensor_copy(out=grouped, in_=abstract_t[:].rearrange("p t r -> p r t"))
        quantise_half(DATA_PASSES)

        acc = [
            psum.tile([TOKENS, N_TILE], F32, tag="bank", name="acc%d" % n)
            for n in range(N_TILES)
        ]
        for i in range(len(pieces)):
            g, first_bank, banks = pieces[i]
            for j in range(banks):
                n = first_bank + j
                nc.tensor.matmul_mx(
                    out=acc[n][:],
                    lhsT=x_codes[:, g * TOKENS : (g + 1) * TOKENS].bitcast(FP8X4),
                    lhsT_scale=x_scales[:, g * TOKENS : (g + 1) * TOKENS],
                    rhs=w_words[i][
                        :, FP4_BYTES * N_TILE * j : FP4_BYTES * N_TILE * (j + 1)
                    ].bitcast(FP4X4),
                    rhs_scale=w_plane[g][:, N_TILE * n : N_TILE * (n + 1)],
                    start=(g == 0),
                    stop=(g == PASSES - 1),
                )
            if i + WORD_BUFS < len(pieces):
                load_piece(i + WORD_BUFS)
            if g == PASSES - 1:
                for n in range(first_bank, first_bank + banks):
                    result = results.tile([TOKENS, N_TILE], F32)
                    if n % 2 == 0:
                        nc.scalar.copy(out=result[:], in_=acc[n][:])
                    else:
                        nc.vector.tensor_copy(out=result[:], in_=acc[n][:])
                    nc.sync.dma_start(
                        out=out_rows[:, N_TILE * n : N_TILE * (n + 1)], in_=result[:]
                    )
